import numpy as np
import ml_dtypes


def mxq(x, axis, fmt="e4m3"):
    dtype, down = {"e4m3": (ml_dtypes.float8_e4m3fn, 7), "e5m2": (ml_dtypes.float8_e5m2, 14)}[fmt]
    v = np.moveaxis(np.asarray(x, np.float32).astype(ml_dtypes.bfloat16).astype(np.float64), axis, -1)
    blocks = v.reshape(v.shape[:-1] + (-1, 32))
    amax = np.abs(blocks).max(-1, keepdims=True)
    byte = np.maximum(np.where(amax > 0, np.frexp(amax)[1] - 1 + 127, 0) - down, 1)
    scale = np.exp2(byte - 127.0)
    codes = (blocks / scale).astype(np.float32).astype(dtype).astype(np.float64)
    return np.moveaxis((codes * scale).reshape(v.shape), -1, axis)


WIDE = False


def mx_kscale(k):
    if not WIDE:
        return np.ones(k)
    levels = np.array([10, -10, 5, -5, 0])
    a = np.random.permutation(np.resize(levels, k // 512 * 4)).reshape(k // 512, 4)
    idx = np.arange(k)
    return np.exp2(a[idx // 512, idx % 128 // 32])


BF16 = ml_dtypes.bfloat16


def bf(x):
    return np.asarray(x, np.float32).astype(BF16)


def f64(x):
    return np.asarray(x).astype(np.float64)


E2M1 = np.array([0.0, 0.5, 1.0, 1.5, 2.0, 3.0, 4.0, 6.0, -0.0, -0.5, -1.0, -1.5, -2.0, -3.0, -4.0, -6.0])


def pack_weight(w, fmt):
    k, n = w.shape
    w = f64(bf(w)).reshape(k // 32, 32, n)
    amax = np.abs(w).max(1)
    if fmt == "e4m3":
        byte = np.frexp(amax)[1] - 1 + 127 - 7
    else:
        mant, ex = np.frexp(amax / 6.0)
        byte = np.where(mant > 0.5, ex, ex - 1) + 127
    byte = np.clip(np.where(amax > 0, byte, 1), 1, 254)
    scaled = (w * np.exp2(127.0 - byte)[:, None, :]).reshape(k, n).astype(np.float32)
    by_word = np.ascontiguousarray(scaled.reshape(k // 512, 128, 4, n).transpose(0, 1, 3, 2))
    if fmt == "e4m3":
        words = by_word.astype(ml_dtypes.float8_e4m3fn).view(np.uint8)
    else:
        c = by_word.astype(ml_dtypes.float4_e2m1fn).view(np.uint8) & 0xF
        words = c[..., 0::2] | (c[..., 1::2] << 4)
    return np.ascontiguousarray(words), np.ascontiguousarray(byte.astype(np.uint8).reshape(k // 512, 16, n))


def unpack_weight(words, scales, fmt):
    g, p, n, _ = words.shape
    if fmt == "e4m3":
        vals = np.ascontiguousarray(words).view(ml_dtypes.float8_e4m3fn).astype(np.float64)
    else:
        nib = np.empty((g, p, n, 4), np.uint8)
        nib[..., 0::2] = words & 0xF
        nib[..., 1::2] = words >> 4
        vals = E2M1[nib]
    vals = vals * np.repeat(np.exp2(scales.astype(np.float64) - 127.0), 8, axis=1)[..., None]
    return vals.transpose(0, 1, 3, 2).reshape(g * 512, n)


NP, NH, NF, NU, B, C, H, W, IN_DIM = 7, 3, 2, 4, 8, 512, 8, 16, 256
S = H * W
EPS = 1e-5
FMT = "e4m3"


def make_bn():
    return bf(np.stack([1.0 + 0.1 * np.random.standard_normal(C), 0.1 * np.random.standard_normal(C),
                        0.1 * np.random.standard_normal(C), np.random.uniform(0.5, 1.5, C)]))


def make_w(col):
    w = np.random.standard_normal((C, col.size)) / np.sqrt(col.size) / col
    return pack_weight(np.ascontiguousarray(w.T), FMT)


def make_nodes(n, s):
    return bf(np.random.standard_normal((n, B, C, H, W)) * s[:, None, None])


def setup_inputs():
    s = mx_kscale(C)
    p_nodes = make_nodes(NP, s)
    h_nodes = make_nodes(NH, s)
    wd_words, wd_scales = make_w(np.concatenate([s, s]))
    bn_decomp_half = make_bn()
    wb_words, wb_scales = make_w(np.concatenate([s, s]))
    bn_bg_p = make_bn()
    return {'p_nodes': p_nodes, 'h_nodes': h_nodes,
            'W_decomp_half_words': wd_words, 'W_decomp_half_scales': wd_scales, 'bn_decomp_half': bn_decomp_half,
            'W_bg_p_words': wb_words, 'W_bg_p_scales': wb_scales, 'bn_bg_p': bn_bg_p}


def conv(wq, xs):
    y, c0 = 0.0, 0
    for x in xs:
        c1 = c0 + x.shape[1]
        y = y + (wq[:, c0:c1] @ x)
        c0 = c1
    return y


def bn_relu(y, bn):
    gamma, beta, mean, var = f64(bn)
    scale = gamma / np.sqrt(var + EPS)
    shift = beta - mean * scale
    return np.maximum(y * scale[:, None] + shift[:, None], 0.0)


def reference(p_nodes, h_nodes, W_decomp_half_words, W_decomp_half_scales, bn_decomp_half, W_bg_p_words, W_bg_p_scales, bn_bg_p):
    pq = mxq(f64(p_nodes).reshape(NP, B, C, S), 2, 'e4m3')
    hq = mxq(f64(h_nodes).reshape(NH, B, C, S), 2, 'e4m3')
    wd = unpack_weight(W_decomp_half_words, W_decomp_half_scales, FMT).T
    wb = unpack_weight(W_bg_p_words, W_bg_p_scales, FMT).T
    p0 = bn_relu(conv(wb, [hq[0], pq[0]]), bn_bg_p)
    p_up = [bn_relu(conv(wd, [hq[1], pq[n]]), bn_decomp_half) for n in range(1, 1 + NU)]
    p_lo = [bn_relu(conv(wd, [hq[2], pq[n]]), bn_decomp_half) for n in range(1 + NU, NP)]
    return np.stack([p0] + p_up + p_lo).reshape(NP, B, C, H, W)

@@ -1,0 +1,185 @@
+from contextlib import ExitStack
+
+import concourse.mybir as mybir
+from concourse.masks import make_identity
+
+F32 = mybir.dt.float32
+BF16 = mybir.dt.bfloat16
+I32 = mybir.dt.int32
+U32 = mybir.dt.uint32
+U8 = mybir.dt.uint8
+FP8X4 = mybir.dt.float8_e4m3fn_x4
+RELU = mybir.ActivationFunctionType.Relu
+
+P = 128
+PACK = 4
+PARTS = 7
+BATCH = 8
+CHANNELS = 512
+PIXELS = 128
+EPS = 1e-5
+
+PARENT_OF_PART = (0, 1, 1, 1, 1, 2, 2)
+WEIGHT_OF_PART = (0, 1, 1, 1, 1, 1, 1)
+WEIGHTS = 2
+K_GROUPS = 2
+
+IMAGES = 4
+COLS = IMAGES * PIXELS
+HALVES = BATCH // IMAGES
+O_TILES = CHANNELS // P
+QUADRANTS = 4
+BN_ROWS = 4
+
+CHUNKS = (PARTS + 3) * HALVES
+RESULT_BUFS = 32
+
+FLOPS = 2 * PARTS * BATCH * PIXELS * CHANNELS * (K_GROUPS * CHANNELS)
+
+
+def load_half_node(nc, pool, node, half):
+    raw = pool.tile([P, IMAGES, PACK * PIXELS], BF16, name="raw")
+    images = node[half * IMAGES : (half + 1) * IMAGES]
+    nc.sync.dma_start(out=raw[:], in_=images.rearrange("b (p j) h w -> p b (j h w)", j=PACK))
+    return raw
+
+
+def quantise_half_node(nc, stage, raw, codes, scales):
+    grouped = stage.tile([P, COLS, PACK], BF16, align_bytes=64, name="grouped")
+    nc.vector.tensor_copy(
+        out=grouped[:].rearrange("p (b c i) j -> p b c j i", b=IMAGES, i=4),
+        in_=raw[:].rearrange("p b (j c i) -> p b c j i", j=PACK, i=4),
+    )
+    nc.vector.quantize_mx(
+        out=codes[:].bitcast(FP8X4),
+        scales=scales[:],
+        in_=grouped[:].rearrange("p w j -> p (w j)"),
+    )
+
+
+def tile_gnn_pb_kernel(
+    tc,
+    p_nodes,
+    h_nodes,
+    W_decomp_half_words,
+    W_decomp_half_scales,
+    bn_decomp_half,
+    W_bg_p_words,
+    W_bg_p_scales,
+    bn_bg_p,
+    out,
+):
+    nc = tc.nc
+    weight_words = (W_bg_p_words, W_decomp_half_words)
+    weight_scales = (W_bg_p_scales, W_decomp_half_scales)
+    batch_norms = (bn_bg_p, bn_decomp_half)
+
+    with ExitStack() as ctx:
+        keep = ctx.enter_context(tc.tile_pool(name="keep", bufs=1))
+        raw_pool = ctx.enter_context(tc.tile_pool(name="raw_pool", bufs=CHUNKS))
+        stage = ctx.enter_context(tc.tile_pool(name="stage", bufs=3))
+        part_pool = ctx.enter_context(tc.tile_pool(name="part_pool", bufs=4))
+        results = ctx.enter_context(tc.tile_pool(name="results", bufs=RESULT_BUFS))
+        banks = ctx.enter_context(tc.psum_pool(name="banks", bufs=7))
+        bn_bank = ctx.enter_context(tc.psum_pool(name="bn_bank", bufs=1))
+
+        w_words = keep.tile([P, WEIGHTS, K_GROUPS, CHANNELS], U32, align_bytes=64)
+        w_scales = keep.tile([P, WEIGHTS, K_GROUPS, CHANNELS], U8, align_bytes=64)
+        nc.vector.memset(w_scales[:].bitcast(I32), 0)
+
+        raw_parent = {}
+        raw_part = {}
+        loaded_weights = set()
+        for part in range(PARTS):
+            parent = PARENT_OF_PART[part]
+            weight = WEIGHT_OF_PART[part]
+            for half in range(HALVES):
+                if (parent, half) not in raw_parent:
+                    raw_parent[(parent, half)] = load_half_node(nc, raw_pool, h_nodes[parent], half)
+                raw_part[(part, half)] = load_half_node(nc, raw_pool, p_nodes[part], half)
+                if weight not in loaded_weights:
+                    loaded_weights.add(weight)
+                    nc.sync.dma_start(
+                        out=w_words[:, weight].bitcast(I32),
+                        in_=weight_words[weight].rearrange("g p n t -> p g (n t)").bitcast(I32),
+                    )
+                    for quadrant in range(QUADRANTS):
+                        rows = weight_scales[weight][:, 4 * quadrant : 4 * quadrant + 4, :]
+                        nc.sync.dma_start(
+                            out=w_scales[32 * quadrant : 32 * quadrant + 4, weight].bitcast(I32),
+                            in_=rows.rearrange("g r n -> r g n").bitcast(I32),
+                        )
+
+        identity = keep.tile([P, P], BF16)
+        make_identity(nc, identity[:])
+        bn_rows = keep.tile([P, P], BF16)
+        nc.vector.memset(bn_rows[:], 0.0)
+        rows_each = BN_ROWS * O_TILES
+        for weight in range(WEIGHTS):
+            nc.scalar.dma_start(
+                out=bn_rows[weight * rows_each : (weight + 1) * rows_each, :],
+                in_=batch_norms[weight].rearrange("r (t m) -> (r t) m", m=P),
+            )
+        bn_turned = bn_bank.tile([P, P], BF16)
+        nc.tensor.transpose(bn_turned[:], bn_rows[:], identity[:])
+        bn_cols = keep.tile([P, WEIGHTS, BN_ROWS, O_TILES], F32)
+        nc.vector.tensor_copy(
+            out=bn_cols[:].rearrange("p w r t -> p (w r t)"), in_=bn_turned[:, 0 : WEIGHTS * rows_each]
+        )
+        gamma, beta, mean, var = (bn_cols[:, :, r, :] for r in range(BN_ROWS))
+        var_eps = keep.tile([P, WEIGHTS, O_TILES], F32)
+        nc.vector.tensor_scalar_add(out=var_eps[:], in0=var, scalar1=EPS)
+        std = keep.tile([P, WEIGHTS, O_TILES], F32)
+        nc.scalar.sqrt(out=std[:], in_=var_eps[:])
+        inv_std = keep.tile([P, WEIGHTS, O_TILES], F32)
+        nc.vector.reciprocal(out=inv_std[:], in_=std[:])
+        bn_scale = keep.tile([P, WEIGHTS, O_TILES], F32)
+        nc.vector.tensor_mul(out=bn_scale[:], in0=gamma, in1=inv_std[:])
+        mean_scaled = keep.tile([P, WEIGHTS, O_TILES], F32)
+        nc.vector.tensor_mul(out=mean_scaled[:], in0=mean, in1=bn_scale[:])
+        bn_shift = keep.tile([P, WEIGHTS, O_TILES], F32)
+        nc.vector.tensor_sub(out=bn_shift[:], in0=beta, in1=mean_scaled[:])
+
+        parent_codes = {}
+        for part in range(PARTS):
+            parent = PARENT_OF_PART[part]
+            weight = WEIGHT_OF_PART[part]
+            for half in range(HALVES):
+                if (parent, half) not in parent_codes:
+                    h_codes = keep.tile([P, COLS], U32, align_bytes=64, name="h_codes_%d_%d" % (parent, half))
+                    h_scales = keep.tile([P, COLS], U8, align_bytes=64, name="h_scales_%d_%d" % (parent, half))
+                    quantise_half_node(nc, stage, raw_parent[(parent, half)], h_codes, h_scales)
+                    parent_codes[(parent, half)] = (h_codes, h_scales)
+                p_codes = part_pool.tile([P, COLS], U32, align_bytes=64)
+                p_scales = part_pool.tile([P, COLS], U8, align_bytes=64)
+                quantise_half_node(nc, stage, raw_part[(part, half)], p_codes, p_scales)
+
+                moving = (parent_codes[(parent, half)], (p_codes, p_scales))
+                for o_tile in range(O_TILES):
+                    o_cols = slice(o_tile * P, (o_tile + 1) * P)
+                    acc = banks.tile([P, COLS], F32)
+                    for g in range(K_GROUPS):
+                        codes, scales = moving[g]
+                        nc.tensor.matmul_mx(
+                            out=acc[:],
+                            lhsT=w_words[:, weight, g, o_cols].bitcast(FP8X4),
+                            lhsT_scale=w_scales[:, weight, g, o_cols],
+                            rhs=codes[:].bitcast(FP8X4),
+                            rhs_scale=scales[:],
+                            start=(g == 0),
+                            stop=(g == K_GROUPS - 1),
+                        )
+                    result = results.tile([P, COLS], F32)
+                    nc.scalar.activation(
+                        out=result[:],
+                        in_=acc[:],
+                        func=RELU,
+                        bias=bn_shift[:, weight, o_tile : o_tile + 1],
+                        scale=bn_scale[:, weight, o_tile : o_tile + 1],
+                    )
+                    nc.scalar.dma_start(
+                        out=out[part, half * IMAGES : (half + 1) * IMAGES, o_cols].rearrange(
+                            "b m h w -> m b (h w)"
+                        ),
+                        in_=result[:].rearrange("m (b s) -> m b s", b=IMAGES),
+                    )

@@ -177,7 +177,8 @@ def tile_gnn_pb_kernel(
                         bias=bn_shift[:, weight, o_tile : o_tile + 1],
                         scale=bn_scale[:, weight, o_tile : o_tile + 1],
                     )
-                    nc.scalar.dma_start(
+                    store_queue = nc.scalar if o_tile % 2 == 0 else nc.sync
+                    store_queue.dma_start(
                         out=out[part, half * IMAGES : (half + 1) * IMAGES, o_cols].rearrange(
                             "b m h w -> m b (h w)"
                         ),

@@ -14,6 +14,7 @@ RELU = mybir.ActivationFunctionType.Relu
 P = 128
 PACK = 4
 PARTS = 7
+PARENTS = 3
 BATCH = 8
 CHANNELS = 512
 PIXELS = 128
@@ -27,11 +28,13 @@ K_GROUPS = 2
 IMAGES = 4
 COLS = IMAGES * PIXELS
 HALVES = BATCH // IMAGES
-O_TILES = CHANNELS // P
+ROUNDS = PARTS * HALVES
+O_SETS = CHANNELS // P
 QUADRANTS = 4
 BN_ROWS = 4
 
-CHUNKS = (PARTS + 3) * HALVES
+AHEAD = 2
+CHUNKS = (PARTS + PARENTS) * HALVES
 RESULT_BUFS = 32
 
 FLOPS = 2 * PARTS * BATCH * PIXELS * CHANNELS * (K_GROUPS * CHANNELS)
@@ -42,19 +45,6 @@ def load_half_node(nc, pool, node, half):
     images = node[half * IMAGES : (half + 1) * IMAGES]
     nc.sync.dma_start(out=raw[:], in_=images.rearrange("b (p j) h w -> p b (j h w)", j=PACK))
     return raw
-
-
-def quantise_half_node(nc, stage, raw, codes, scales):
-    grouped = stage.tile([P, COLS, PACK], BF16, align_bytes=64, name="grouped")
-    nc.vector.tensor_copy(
-        out=grouped[:].rearrange("p (b c i) j -> p b c j i", b=IMAGES, i=4),
-        in_=raw[:].rearrange("p b (j c i) -> p b c j i", j=PACK, i=4),
-    )
-    nc.vector.quantize_mx(
-        out=codes[:].bitcast(FP8X4),
-        scales=scales[:],
-        in_=grouped[:].rearrange("p w j -> p (w j)"),
-    )
 
 
 def tile_gnn_pb_kernel(
@@ -77,11 +67,10 @@ def tile_gnn_pb_kernel(
     with ExitStack() as ctx:
         keep = ctx.enter_context(tc.tile_pool(name="keep", bufs=1))
         raw_pool = ctx.enter_context(tc.tile_pool(name="raw_pool", bufs=CHUNKS))
-        stage = ctx.enter_context(tc.tile_pool(name="stage", bufs=3))
-        part_pool = ctx.enter_context(tc.tile_pool(name="part_pool", bufs=4))
+        stage = ctx.enter_context(tc.tile_pool(name="stage", bufs=4))
+        part_pool = ctx.enter_context(tc.tile_pool(name="part_pool", bufs=AHEAD + 2))
+        sorted_pool = ctx.enter_context(tc.tile_pool(name="sorted_pool", bufs=2 * IMAGES))
         results = ctx.enter_context(tc.tile_pool(name="results", bufs=RESULT_BUFS))
-        banks = ctx.enter_context(tc.psum_pool(name="banks", bufs=7))
-        bn_bank = ctx.enter_context(tc.psum_pool(name="bn_bank", bufs=1))
 
         w_words = keep.tile([P, WEIGHTS, K_GROUPS, CHANNELS], U32, align_bytes=64)
         w_scales = keep.tile([P, WEIGHTS, K_GROUPS, CHANNELS], U8, align_bytes=64)
@@ -90,97 +79,167 @@ def tile_gnn_pb_kernel(
         raw_parent = {}
         raw_part = {}
         loaded_weights = set()
-        for part in range(PARTS):
+        for r in range(ROUNDS):
+            part, half = divmod(r, HALVES)
             parent = PARENT_OF_PART[part]
             weight = WEIGHT_OF_PART[part]
-            for half in range(HALVES):
-                if (parent, half) not in raw_parent:
-                    raw_parent[(parent, half)] = load_half_node(nc, raw_pool, h_nodes[parent], half)
-                raw_part[(part, half)] = load_half_node(nc, raw_pool, p_nodes[part], half)
-                if weight not in loaded_weights:
-                    loaded_weights.add(weight)
+            if (parent, half) not in raw_parent:
+                raw_parent[(parent, half)] = load_half_node(nc, raw_pool, h_nodes[parent], half)
+            raw_part[r] = load_half_node(nc, raw_pool, p_nodes[part], half)
+            if weight not in loaded_weights:
+                loaded_weights.add(weight)
+                nc.sync.dma_start(
+                    out=w_words[:, weight].bitcast(I32),
+                    in_=weight_words[weight].rearrange("g p n t -> p g (n t)").bitcast(I32),
+                )
+                for quadrant in range(QUADRANTS):
+                    rows = weight_scales[weight][:, 4 * quadrant : 4 * quadrant + 4, :]
                     nc.sync.dma_start(
-                        out=w_words[:, weight].bitcast(I32),
-                        in_=weight_words[weight].rearrange("g p n t -> p g (n t)").bitcast(I32),
+                        out=w_scales[32 * quadrant : 32 * quadrant + 4, weight].bitcast(I32),
+                        in_=rows.rearrange("g r n -> r g n").bitcast(I32),
                     )
-                    for quadrant in range(QUADRANTS):
-                        rows = weight_scales[weight][:, 4 * quadrant : 4 * quadrant + 4, :]
-                        nc.sync.dma_start(
-                            out=w_scales[32 * quadrant : 32 * quadrant + 4, weight].bitcast(I32),
-                            in_=rows.rearrange("g r n -> r g n").bitcast(I32),
-                        )
 
-        identity = keep.tile([P, P], BF16)
+        identity = keep.tile([P, P], F32)
         make_identity(nc, identity[:])
-        bn_rows = keep.tile([P, P], BF16)
+        bn_rows = keep.tile([P, CHANNELS], BF16)
         nc.vector.memset(bn_rows[:], 0.0)
-        rows_each = BN_ROWS * O_TILES
         for weight in range(WEIGHTS):
             nc.scalar.dma_start(
-                out=bn_rows[weight * rows_each : (weight + 1) * rows_each, :],
-                in_=batch_norms[weight].rearrange("r (t m) -> (r t) m", m=P),
+                out=bn_rows[weight * BN_ROWS : (weight + 1) * BN_ROWS, :], in_=batch_norms[weight]
             )
-        bn_turned = bn_bank.tile([P, P], BF16)
-        nc.tensor.transpose(bn_turned[:], bn_rows[:], identity[:])
-        bn_cols = keep.tile([P, WEIGHTS, BN_ROWS, O_TILES], F32)
-        nc.vector.tensor_copy(
-            out=bn_cols[:].rearrange("p w r t -> p (w r t)"), in_=bn_turned[:, 0 : WEIGHTS * rows_each]
-        )
-        gamma, beta, mean, var = (bn_cols[:, :, r, :] for r in range(BN_ROWS))
-        var_eps = keep.tile([P, WEIGHTS, O_TILES], F32)
+        bn_sorted = keep.tile([P, O_SETS, P], F32)
+        nc.vector.tensor_copy(out=bn_sorted[:], in_=bn_rows[:].rearrange("p (m j) -> p j m", j=O_SETS))
+        bn_cols = keep.tile([P, O_SETS, WEIGHTS, BN_ROWS], F32)
+        with tc.psum_pool(name="bn_bank", bufs=1) as bn_bank:
+            bn_turned = bn_bank.tile([P, O_SETS, P], F32)
+            for j in range(O_SETS):
+                nc.tensor.transpose(bn_turned[:, j, :], bn_sorted[:, j, :], identity[:])
+            nc.vector.tensor_copy(
+                out=bn_cols[:].rearrange("p j w r -> p j (w r)"),
+                in_=bn_turned[:, :, 0 : WEIGHTS * BN_ROWS],
+            )
+        gamma, beta, mean, var = (bn_cols[:, :, :, row] for row in range(BN_ROWS))
+        var_eps = keep.tile([P, O_SETS, WEIGHTS], F32)
         nc.vector.tensor_scalar_add(out=var_eps[:], in0=var, scalar1=EPS)
-        std = keep.tile([P, WEIGHTS, O_TILES], F32)
+        std = keep.tile([P, O_SETS, WEIGHTS], F32)
         nc.scalar.sqrt(out=std[:], in_=var_eps[:])
-        inv_std = keep.tile([P, WEIGHTS, O_TILES], F32)
+        inv_std = keep.tile([P, O_SETS, WEIGHTS], F32)
         nc.vector.reciprocal(out=inv_std[:], in_=std[:])
-        bn_scale = keep.tile([P, WEIGHTS, O_TILES], F32)
+        bn_scale = keep.tile([P, O_SETS, WEIGHTS], F32)
         nc.vector.tensor_mul(out=bn_scale[:], in0=gamma, in1=inv_std[:])
-        mean_scaled = keep.tile([P, WEIGHTS, O_TILES], F32)
+        mean_scaled = keep.tile([P, O_SETS, WEIGHTS], F32)
         nc.vector.tensor_mul(out=mean_scaled[:], in0=mean, in1=bn_scale[:])
-        bn_shift = keep.tile([P, WEIGHTS, O_TILES], F32)
+        bn_shift = keep.tile([P, O_SETS, WEIGHTS], F32)
         nc.vector.tensor_sub(out=bn_shift[:], in0=beta, in1=mean_scaled[:])
 
+        sum_banks = ctx.enter_context(tc.psum_pool(name="sum_banks", bufs=IMAGES))
+        turn_banks = ctx.enter_context(tc.psum_pool(name="turn_banks", bufs=IMAGES))
+        to_quantise = {}
         parent_codes = {}
-        for part in range(PARTS):
-            parent = PARENT_OF_PART[part]
-            weight = WEIGHT_OF_PART[part]
-            for half in range(HALVES):
-                if (parent, half) not in parent_codes:
-                    h_codes = keep.tile([P, COLS], U32, align_bytes=64, name="h_codes_%d_%d" % (parent, half))
-                    h_scales = keep.tile([P, COLS], U8, align_bytes=64, name="h_scales_%d_%d" % (parent, half))
-                    quantise_half_node(nc, stage, raw_parent[(parent, half)], h_codes, h_scales)
-                    parent_codes[(parent, half)] = (h_codes, h_scales)
-                p_codes = part_pool.tile([P, COLS], U32, align_bytes=64)
-                p_scales = part_pool.tile([P, COLS], U8, align_bytes=64)
-                quantise_half_node(nc, stage, raw_part[(part, half)], p_codes, p_scales)
+        part_codes = {}
+        sums = {}
+        sorted_sums = {}
+        turned = {}
 
-                moving = (parent_codes[(parent, half)], (p_codes, p_scales))
-                for o_tile in range(O_TILES):
-                    o_cols = slice(o_tile * P, (o_tile + 1) * P)
-                    acc = banks.tile([P, COLS], F32)
-                    for g in range(K_GROUPS):
-                        codes, scales = moving[g]
-                        nc.tensor.matmul_mx(
-                            out=acc[:],
-                            lhsT=w_words[:, weight, g, o_cols].bitcast(FP8X4),
-                            lhsT_scale=w_scales[:, weight, g, o_cols],
-                            rhs=codes[:].bitcast(FP8X4),
-                            rhs_scale=scales[:],
-                            start=(g == 0),
-                            stop=(g == K_GROUPS - 1),
-                        )
-                    result = results.tile([P, COLS], F32)
+        def regroup(r):
+            part, half = divmod(r, HALVES)
+            parent = PARENT_OF_PART[part]
+            jobs = []
+            if (parent, half) not in parent_codes:
+                h_codes = keep.tile([P, COLS], U32, align_bytes=64, name="h_codes_%d_%d" % (parent, half))
+                h_scales = keep.tile([P, COLS], U8, align_bytes=64, name="h_scales_%d_%d" % (parent, half))
+                parent_codes[(parent, half)] = (h_codes, h_scales)
+                jobs.append((raw_parent[(parent, half)], h_codes, h_scales))
+            p_codes = part_pool.tile([P, COLS], U32, align_bytes=64, name="p_codes")
+            p_scales = part_pool.tile([P, COLS], U8, align_bytes=64, name="p_scales")
+            part_codes[r] = (p_codes, p_scales)
+            jobs.append((raw_part[r], p_codes, p_scales))
+            to_quantise[r] = []
+            for raw, codes, scales in jobs:
+                grouped = stage.tile([P, COLS, PACK], BF16, align_bytes=64, name="grouped")
+                nc.vector.tensor_copy(
+                    out=grouped[:].rearrange("p (b c i) j -> p b c j i", b=IMAGES, i=4),
+                    in_=raw[:].rearrange("p b (j c i) -> p b c j i", j=PACK, i=4),
+                )
+                to_quantise[r].append((grouped, codes, scales))
+
+        def quantise(r):
+            for grouped, codes, scales in to_quantise[r]:
+                nc.vector.quantize_mx(
+                    out=codes[:].bitcast(FP8X4),
+                    scales=scales[:],
+                    in_=grouped[:].rearrange("p w j -> p (w j)"),
+                )
+
+        def multiply(r):
+            part, half = divmod(r, HALVES)
+            weight = WEIGHT_OF_PART[part]
+            operands = (parent_codes[(PARENT_OF_PART[part], half)], part_codes[r])
+            for image in range(IMAGES):
+                pixels = slice(image * PIXELS, (image + 1) * PIXELS)
+                acc = sum_banks.tile([P, CHANNELS], F32, name="acc")
+                for g in range(K_GROUPS):
+                    codes, scales = operands[g]
+                    nc.tensor.matmul_mx(
+                        out=acc[:],
+                        lhsT=codes[:, pixels].bitcast(FP8X4),
+                        lhsT_scale=scales[:, pixels],
+                        rhs=w_words[:, weight, g, :].bitcast(FP8X4),
+                        rhs_scale=w_scales[:, weight, g, :],
+                        start=(g == 0),
+                        stop=(g == K_GROUPS - 1),
+                    )
+                sums[(r, image)] = acc
+
+        def sort_channels(r, image):
+            tidy = sorted_pool.tile([P, O_SETS, P], F32, name="tidy")
+            by_set = sums[(r, image)][:].rearrange("s (m j) -> s j m", j=O_SETS)
+            if image % 2 == 0:
+                nc.vector.tensor_copy(out=tidy[:], in_=by_set)
+            else:
+                nc.scalar.copy(out=tidy[:], in_=by_set)
+            sorted_sums[(r, image)] = tidy
+
+        def turn(r):
+            for image in range(IMAGES):
+                bank = turn_banks.tile([P, O_SETS, PIXELS], F32, name="bank")
+                for j in range(O_SETS):
+                    nc.tensor.transpose(bank[:, j, :], sorted_sums[(r, image)][:, j, :], identity[:])
+                turned[(r, image)] = bank
+
+        def finish(r):
+            part, half = divmod(r, HALVES)
+            weight = WEIGHT_OF_PART[part]
+            for image in range(IMAGES):
+                result = results.tile([P, O_SETS, PIXELS], F32, name="result")
+                for j in range(O_SETS):
                     nc.scalar.activation(
-                        out=result[:],
-                        in_=acc[:],
+                        out=result[:, j, :],
+                        in_=turned[(r, image)][:, j, :],
                         func=RELU,
-                        bias=bn_shift[:, weight, o_tile : o_tile + 1],
-                        scale=bn_scale[:, weight, o_tile : o_tile + 1],
+                        bias=bn_shift[:, j, weight : weight + 1],
+                        scale=bn_scale[:, j, weight : weight + 1],
                     )
-                    store_queue = nc.scalar if o_tile % 2 == 0 else nc.sync
-                    store_queue.dma_start(
-                        out=out[part, half * IMAGES : (half + 1) * IMAGES, o_cols].rearrange(
-                            "b m h w -> m b (h w)"
-                        ),
-                        in_=result[:].rearrange("m (b s) -> m b s", b=IMAGES),
-                    )
+                nc.sync.dma_start(
+                    out=out[part, half * IMAGES + image].rearrange("(m j) h w -> m (j h w)", j=O_SETS),
+                    in_=result[:].rearrange("m j s -> m (j s)"),
+                )
+
+        with tc.manual_schedule():
+            for r in range(AHEAD):
+                regroup(r)
+                quantise(r)
+            for r in range(ROUNDS + 1):
+                if r < ROUNDS:
+                    multiply(r)
+                    sort_channels(r, 0)
+                    sort_channels(r, 1)
+                    if r + AHEAD < ROUNDS:
+                        regroup(r + AHEAD)
+                    sort_channels(r, 2)
+                    sort_channels(r, 3)
+                    if r + AHEAD < ROUNDS:
+                        quantise(r + AHEAD)
+                if r >= 1:
+                    turn(r - 1)
+                    finish(r - 1)

@@ -35,7 +35,7 @@ BN_ROWS = 4
 
 AHEAD = 2
 CHUNKS = (PARTS + PARENTS) * HALVES
-RESULT_BUFS = 32
+RESULT_BUFS = 8
 
 FLOPS = 2 * PARTS * BATCH * PIXELS * CHANNELS * (K_GROUPS * CHANNELS)
 
@@ -201,29 +201,30 @@ def tile_gnn_pb_kernel(
             sorted_sums[(r, image)] = tidy
 
         def turn(r):
-            for image in range(IMAGES):
-                bank = turn_banks.tile([P, O_SETS, PIXELS], F32, name="bank")
-                for j in range(O_SETS):
-                    nc.tensor.transpose(bank[:, j, :], sorted_sums[(r, image)][:, j, :], identity[:])
-                turned[(r, image)] = bank
+            for j in range(O_SETS):
+                bank = turn_banks.tile([P, IMAGES, PIXELS], F32, name="bank")
+                for image in range(IMAGES):
+                    nc.tensor.transpose(bank[:, image, :], sorted_sums[(r, image)][:, j, :], identity[:])
+                turned[(r, j)] = bank
 
         def finish(r):
             part, half = divmod(r, HALVES)
             weight = WEIGHT_OF_PART[part]
-            for image in range(IMAGES):
-                result = results.tile([P, O_SETS, PIXELS], F32, name="result")
-                for j in range(O_SETS):
-                    nc.scalar.activation(
-                        out=result[:, j, :],
-                        in_=turned[(r, image)][:, j, :],
-                        func=RELU,
-                        bias=bn_shift[:, j, weight : weight + 1],
-                        scale=bn_scale[:, j, weight : weight + 1],
-                    )
-                nc.sync.dma_start(
-                    out=out[part, half * IMAGES + image].rearrange("(m j) h w -> m (j h w)", j=O_SETS),
-                    in_=result[:].rearrange("m j s -> m (j s)"),
+            result = results.tile([P, IMAGES, O_SETS, PIXELS], F32, name="result")
+            for j in range(O_SETS):
+                nc.scalar.activation(
+                    out=result[:, :, j, :],
+                    in_=turned[(r, j)][:],
+                    func=RELU,
+                    bias=bn_shift[:, j, weight : weight + 1],
+                    scale=bn_scale[:, j, weight : weight + 1],
                 )
+            nc.sync.dma_start(
+                out=out[part, half * IMAGES : (half + 1) * IMAGES].rearrange(
+                    "b (m j) h w -> m b (j h w)", j=O_SETS
+                ),
+                in_=result[:].rearrange("m b j s -> m b (j s)"),
+            )
 
         with tc.manual_schedule():
             for r in range(AHEAD):

@@ -33,9 +33,8 @@ O_SETS = CHANNELS // P
 QUADRANTS = 4
 BN_ROWS = 4
 
-AHEAD = 2
 CHUNKS = (PARTS + PARENTS) * HALVES
-RESULT_BUFS = 8
+RESULT_BUFS = 32
 
 FLOPS = 2 * PARTS * BATCH * PIXELS * CHANNELS * (K_GROUPS * CHANNELS)
 
@@ -68,7 +67,7 @@ def tile_gnn_pb_kernel(
         keep = ctx.enter_context(tc.tile_pool(name="keep", bufs=1))
         raw_pool = ctx.enter_context(tc.tile_pool(name="raw_pool", bufs=CHUNKS))
         stage = ctx.enter_context(tc.tile_pool(name="stage", bufs=4))
-        part_pool = ctx.enter_context(tc.tile_pool(name="part_pool", bufs=AHEAD + 2))
+        part_pool = ctx.enter_context(tc.tile_pool(name="part_pool", bufs=3))
         sorted_pool = ctx.enter_context(tc.tile_pool(name="sorted_pool", bufs=2 * IMAGES))
         results = ctx.enter_context(tc.tile_pool(name="results", bufs=RESULT_BUFS))
 
@@ -83,21 +82,23 @@ def tile_gnn_pb_kernel(
             part, half = divmod(r, HALVES)
             parent = PARENT_OF_PART[part]
             weight = WEIGHT_OF_PART[part]
-            if (parent, half) not in raw_parent:
-                raw_parent[(parent, half)] = load_half_node(nc, raw_pool, h_nodes[parent], half)
-            raw_part[r] = load_half_node(nc, raw_pool, p_nodes[part], half)
-            if weight not in loaded_weights:
+            new_weight = weight not in loaded_weights
+            if new_weight:
                 loaded_weights.add(weight)
-                nc.sync.dma_start(
-                    out=w_words[:, weight].bitcast(I32),
-                    in_=weight_words[weight].rearrange("g p n t -> p g (n t)").bitcast(I32),
-                )
                 for quadrant in range(QUADRANTS):
                     rows = weight_scales[weight][:, 4 * quadrant : 4 * quadrant + 4, :]
                     nc.sync.dma_start(
                         out=w_scales[32 * quadrant : 32 * quadrant + 4, weight].bitcast(I32),
                         in_=rows.rearrange("g r n -> r g n").bitcast(I32),
                     )
+            if (parent, half) not in raw_parent:
+                raw_parent[(parent, half)] = load_half_node(nc, raw_pool, h_nodes[parent], half)
+            raw_part[r] = load_half_node(nc, raw_pool, p_nodes[part], half)
+            if new_weight:
+                nc.sync.dma_start(
+                    out=w_words[:, weight].bitcast(I32),
+                    in_=weight_words[weight].rearrange("g p n t -> p g (n t)").bitcast(I32),
+                )
 
         identity = keep.tile([P, P], F32)
         make_identity(nc, identity[:])
@@ -201,46 +202,45 @@ def tile_gnn_pb_kernel(
             sorted_sums[(r, image)] = tidy
 
         def turn(r):
-            for j in range(O_SETS):
-                bank = turn_banks.tile([P, IMAGES, PIXELS], F32, name="bank")
-                for image in range(IMAGES):
-                    nc.tensor.transpose(bank[:, image, :], sorted_sums[(r, image)][:, j, :], identity[:])
-                turned[(r, j)] = bank
+            for image in range(IMAGES):
+                bank = turn_banks.tile([P, O_SETS, PIXELS], F32, name="bank")
+                for j in range(O_SETS):
+                    nc.tensor.transpose(bank[:, j, :], sorted_sums[(r, image)][:, j, :], identity[:])
+                turned[(r, image)] = bank
 
         def finish(r):
             part, half = divmod(r, HALVES)
             weight = WEIGHT_OF_PART[part]
-            result = results.tile([P, IMAGES, O_SETS, PIXELS], F32, name="result")
-            for j in range(O_SETS):
-                nc.scalar.activation(
-                    out=result[:, :, j, :],
-                    in_=turned[(r, j)][:],
-                    func=RELU,
-                    bias=bn_shift[:, j, weight : weight + 1],
-                    scale=bn_scale[:, j, weight : weight + 1],
+            for image in range(IMAGES):
+                result = results.tile([P, O_SETS, PIXELS], F32, name="result")
+                for j in range(O_SETS):
+                    nc.scalar.activation(
+                        out=result[:, j, :],
+                        in_=turned[(r, image)][:, j, :],
+                        func=RELU,
+                        bias=bn_shift[:, j, weight : weight + 1],
+                        scale=bn_scale[:, j, weight : weight + 1],
+                    )
+                nc.sync.dma_start(
+                    out=out[part, half * IMAGES + image].rearrange("(m j) h w -> m (j h w)", j=O_SETS),
+                    in_=result[:].rearrange("m j s -> m (j s)"),
                 )
-            nc.sync.dma_start(
-                out=out[part, half * IMAGES : (half + 1) * IMAGES].rearrange(
-                    "b (m j) h w -> m b (j h w)", j=O_SETS
-                ),
-                in_=result[:].rearrange("m b j s -> m b (j s)"),
-            )
 
         with tc.manual_schedule():
-            for r in range(AHEAD):
-                regroup(r)
-                quantise(r)
+            regroup(0)
+            quantise(0)
             for r in range(ROUNDS + 1):
+                if r + 1 < ROUNDS:
+                    regroup(r + 1)
                 if r < ROUNDS:
                     multiply(r)
                     sort_channels(r, 0)
                     sort_channels(r, 1)
-                    if r + AHEAD < ROUNDS:
-                        regroup(r + AHEAD)
+                if r + 1 < ROUNDS:
+                    quantise(r + 1)
+                if r < ROUNDS:
                     sort_channels(r, 2)
                     sort_channels(r, 3)
-                    if r + AHEAD < ROUNDS:
-                        quantise(r + AHEAD)
                 if r >= 1:
                     turn(r - 1)
                     finish(r - 1)

@@ -34,7 +34,7 @@ QUADRANTS = 4
 BN_ROWS = 4
 
 CHUNKS = (PARTS + PARENTS) * HALVES
-RESULT_BUFS = 32
+RESULT_BUFS = 10
 
 FLOPS = 2 * PARTS * BATCH * PIXELS * CHANNELS * (K_GROUPS * CHANNELS)
 
@@ -67,13 +67,14 @@ def tile_gnn_pb_kernel(
         keep = ctx.enter_context(tc.tile_pool(name="keep", bufs=1))
         raw_pool = ctx.enter_context(tc.tile_pool(name="raw_pool", bufs=CHUNKS))
         stage = ctx.enter_context(tc.tile_pool(name="stage", bufs=4))
-        part_pool = ctx.enter_context(tc.tile_pool(name="part_pool", bufs=3))
-        sorted_pool = ctx.enter_context(tc.tile_pool(name="sorted_pool", bufs=2 * IMAGES))
+        part_pool = ctx.enter_context(tc.tile_pool(name="part_pool", bufs=4))
         results = ctx.enter_context(tc.tile_pool(name="results", bufs=RESULT_BUFS))
 
+        arrived_words = keep.tile([P, WEIGHTS, K_GROUPS, CHANNELS], U32, align_bytes=64)
+        arrived_scales = keep.tile([P, WEIGHTS, K_GROUPS, CHANNELS], U8, align_bytes=64)
         w_words = keep.tile([P, WEIGHTS, K_GROUPS, CHANNELS], U32, align_bytes=64)
         w_scales = keep.tile([P, WEIGHTS, K_GROUPS, CHANNELS], U8, align_bytes=64)
-        nc.vector.memset(w_scales[:].bitcast(I32), 0)
+        nc.vector.memset(arrived_scales[:].bitcast(I32), 0)
 
         raw_parent = {}
         raw_part = {}
@@ -82,21 +83,19 @@ def tile_gnn_pb_kernel(
             part, half = divmod(r, HALVES)
             parent = PARENT_OF_PART[part]
             weight = WEIGHT_OF_PART[part]
-            new_weight = weight not in loaded_weights
-            if new_weight:
+            if (parent, half) not in raw_parent:
+                raw_parent[(parent, half)] = load_half_node(nc, raw_pool, h_nodes[parent], half)
+            raw_part[r] = load_half_node(nc, raw_pool, p_nodes[part], half)
+            if weight not in loaded_weights:
                 loaded_weights.add(weight)
                 for quadrant in range(QUADRANTS):
                     rows = weight_scales[weight][:, 4 * quadrant : 4 * quadrant + 4, :]
                     nc.sync.dma_start(
-                        out=w_scales[32 * quadrant : 32 * quadrant + 4, weight].bitcast(I32),
+                        out=arrived_scales[32 * quadrant : 32 * quadrant + 4, weight].bitcast(I32),
                         in_=rows.rearrange("g r n -> r g n").bitcast(I32),
                     )
-            if (parent, half) not in raw_parent:
-                raw_parent[(parent, half)] = load_half_node(nc, raw_pool, h_nodes[parent], half)
-            raw_part[r] = load_half_node(nc, raw_pool, p_nodes[part], half)
-            if new_weight:
                 nc.sync.dma_start(
-                    out=w_words[:, weight].bitcast(I32),
+                    out=arrived_words[:, weight].bitcast(I32),
                     in_=weight_words[weight].rearrange("g p n t -> p g (n t)").bitcast(I32),
                 )
 
@@ -133,14 +132,20 @@ def tile_gnn_pb_kernel(
         bn_shift = keep.tile([P, O_SETS, WEIGHTS], F32)
         nc.vector.tensor_sub(out=bn_shift[:], in0=beta, in1=mean_scaled[:])
 
-        sum_banks = ctx.enter_context(tc.psum_pool(name="sum_banks", bufs=IMAGES))
-        turn_banks = ctx.enter_context(tc.psum_pool(name="turn_banks", bufs=IMAGES))
+        sum_banks = ctx.enter_context(tc.psum_pool(name="sum_banks", bufs=2 * O_SETS))
         to_quantise = {}
         parent_codes = {}
         part_codes = {}
-        sums = {}
-        sorted_sums = {}
-        turned = {}
+
+        def sort_weight(weight):
+            nc.vector.tensor_copy(
+                out=w_scales[:, weight].rearrange("p g (j m) -> p g m j", j=O_SETS),
+                in_=arrived_scales[:, weight].rearrange("p g (m j) -> p g m j", j=O_SETS),
+            )
+            nc.vector.tensor_copy(
+                out=w_words[:, weight].bitcast(I32).rearrange("p g (j m) -> p g j m", j=O_SETS),
+                in_=arrived_words[:, weight].bitcast(I32).rearrange("p g (m j) -> p g j m", j=O_SETS),
+            )
 
         def regroup(r):
             part, half = divmod(r, HALVES)
@@ -172,75 +177,48 @@ def tile_gnn_pb_kernel(
                     in_=grouped[:].rearrange("p w j -> p (w j)"),
                 )
 
-        def multiply(r):
+        def multiply_and_finish(r):
             part, half = divmod(r, HALVES)
             weight = WEIGHT_OF_PART[part]
             operands = (parent_codes[(PARENT_OF_PART[part], half)], part_codes[r])
-            for image in range(IMAGES):
-                pixels = slice(image * PIXELS, (image + 1) * PIXELS)
-                acc = sum_banks.tile([P, CHANNELS], F32, name="acc")
+            result = results.tile([P, IMAGES, O_SETS, PIXELS], F32, name="result")
+            for j in range(O_SETS):
+                channels = slice(j * P, (j + 1) * P)
+                acc = sum_banks.tile([P, COLS], F32, name="acc")
                 for g in range(K_GROUPS):
                     codes, scales = operands[g]
                     nc.tensor.matmul_mx(
                         out=acc[:],
-                        lhsT=codes[:, pixels].bitcast(FP8X4),
-                        lhsT_scale=scales[:, pixels],
-                        rhs=w_words[:, weight, g, :].bitcast(FP8X4),
-                        rhs_scale=w_scales[:, weight, g, :],
+                        lhsT=w_words[:, weight, g, channels].bitcast(FP8X4),
+                        lhsT_scale=w_scales[:, weight, g, channels],
+                        rhs=codes[:].bitcast(FP8X4),
+                        rhs_scale=scales[:],
                         start=(g == 0),
                         stop=(g == K_GROUPS - 1),
                     )
-                sums[(r, image)] = acc
-
-        def sort_channels(r, image):
-            tidy = sorted_pool.tile([P, O_SETS, P], F32, name="tidy")
-            by_set = sums[(r, image)][:].rearrange("s (m j) -> s j m", j=O_SETS)
-            if image % 2 == 0:
-                nc.vector.tensor_copy(out=tidy[:], in_=by_set)
-            else:
-                nc.scalar.copy(out=tidy[:], in_=by_set)
-            sorted_sums[(r, image)] = tidy
-
-        def turn(r):
-            for image in range(IMAGES):
-                bank = turn_banks.tile([P, O_SETS, PIXELS], F32, name="bank")
-                for j in range(O_SETS):
-                    nc.tensor.transpose(bank[:, j, :], sorted_sums[(r, image)][:, j, :], identity[:])
-                turned[(r, image)] = bank
-
-        def finish(r):
-            part, half = divmod(r, HALVES)
-            weight = WEIGHT_OF_PART[part]
-            for image in range(IMAGES):
-                result = results.tile([P, O_SETS, PIXELS], F32, name="result")
-                for j in range(O_SETS):
-                    nc.scalar.activation(
-                        out=result[:, j, :],
-                        in_=turned[(r, image)][:, j, :],
-                        func=RELU,
-                        bias=bn_shift[:, j, weight : weight + 1],
-                        scale=bn_scale[:, j, weight : weight + 1],
-                    )
-                nc.sync.dma_start(
-                    out=out[part, half * IMAGES + image].rearrange("(m j) h w -> m (j h w)", j=O_SETS),
-                    in_=result[:].rearrange("m j s -> m (j s)"),
+                nc.scalar.activation(
+                    out=result[:, :, j, :],
+                    in_=acc[:].rearrange("m (b s) -> m b s", b=IMAGES),
+                    func=RELU,
+                    bias=bn_shift[:, j, weight : weight + 1],
+                    scale=bn_scale[:, j, weight : weight + 1],
                 )
+            nc.sync.dma_start(
+                out=out[part, half * IMAGES : (half + 1) * IMAGES].rearrange(
+                    "b (m j) h w -> m b (j h w)", j=O_SETS
+                ),
+                in_=result[:].rearrange("m b j s -> m b (j s)"),
+            )
 
         with tc.manual_schedule():
+            sorted_weights = set()
             regroup(0)
-            quantise(0)
-            for r in range(ROUNDS + 1):
+            for r in range(ROUNDS):
                 if r + 1 < ROUNDS:
                     regroup(r + 1)
-                if r < ROUNDS:
-                    multiply(r)
-                    sort_channels(r, 0)
-                    sort_channels(r, 1)
-                if r + 1 < ROUNDS:
-                    quantise(r + 1)
-                if r < ROUNDS:
-                    sort_channels(r, 2)
-                    sort_channels(r, 3)
-                if r >= 1:
-                    turn(r - 1)
-                    finish(r - 1)
+                weight = WEIGHT_OF_PART[r // HALVES]
+                if weight not in sorted_weights:
+                    sorted_weights.add(weight)
+                    sort_weight(weight)
+                quantise(r)
+                multiply_and_finish(r)

@@ -203,7 +203,7 @@ def tile_gnn_pb_kernel(
                     bias=bn_shift[:, j, weight : weight + 1],
                     scale=bn_scale[:, j, weight : weight + 1],
                 )
-            nc.sync.dma_start(
+            nc.scalar.dma_start(
                 out=out[part, half * IMAGES : (half + 1) * IMAGES].rearrange(
                     "b (m j) h w -> m b (j h w)", j=O_SETS
                 ),

@@ -34,13 +34,14 @@ QUADRANTS = 4
 BN_ROWS = 4
 
 CHUNKS = (PARTS + PARENTS) * HALVES
+DMA_ALIGN = 256
 RESULT_BUFS = 10
 
 FLOPS = 2 * PARTS * BATCH * PIXELS * CHANNELS * (K_GROUPS * CHANNELS)
 
 
 def load_half_node(nc, pool, node, half):
-    raw = pool.tile([P, IMAGES, PACK * PIXELS], BF16, name="raw")
+    raw = pool.tile([P, IMAGES, PACK * PIXELS], BF16, align_bytes=DMA_ALIGN, name="raw")
     images = node[half * IMAGES : (half + 1) * IMAGES]
     nc.sync.dma_start(out=raw[:], in_=images.rearrange("b (p j) h w -> p b (j h w)", j=PACK))
     return raw
@@ -70,7 +71,7 @@ def tile_gnn_pb_kernel(
         part_pool = ctx.enter_context(tc.tile_pool(name="part_pool", bufs=4))
         results = ctx.enter_context(tc.tile_pool(name="results", bufs=RESULT_BUFS))
 
-        arrived_words = keep.tile([P, WEIGHTS, K_GROUPS, CHANNELS], U32, align_bytes=64)
+        arrived_words = keep.tile([P, WEIGHTS, K_GROUPS, CHANNELS], U32, align_bytes=DMA_ALIGN)
         arrived_scales = keep.tile([P, WEIGHTS, K_GROUPS, CHANNELS], U8, align_bytes=64)
         w_words = keep.tile([P, WEIGHTS, K_GROUPS, CHANNELS], U32, align_bytes=64)
         w_scales = keep.tile([P, WEIGHTS, K_GROUPS, CHANNELS], U8, align_bytes=64)
@@ -181,7 +182,7 @@ def tile_gnn_pb_kernel(
             part, half = divmod(r, HALVES)
             weight = WEIGHT_OF_PART[part]
             operands = (parent_codes[(PARENT_OF_PART[part], half)], part_codes[r])
-            result = results.tile([P, IMAGES, O_SETS, PIXELS], F32, name="result")
+            result = results.tile([P, IMAGES, O_SETS, PIXELS], F32, align_bytes=DMA_ALIGN, name="result")
             for j in range(O_SETS):
                 channels = slice(j * P, (j + 1) * P)
                 acc = sum_banks.tile([P, COLS], F32, name="acc")

@@ -33,17 +33,16 @@ O_SETS = CHANNELS // P
 QUADRANTS = 4
 BN_ROWS = 4
 
-CHUNKS = (PARTS + PARENTS) * HALVES
+NODES = PARTS + PARENTS
 DMA_ALIGN = 256
-RESULT_BUFS = 10
+RESULT_BUFS = 5
 
 FLOPS = 2 * PARTS * BATCH * PIXELS * CHANNELS * (K_GROUPS * CHANNELS)
 
 
-def load_half_node(nc, pool, node, half):
-    raw = pool.tile([P, IMAGES, PACK * PIXELS], BF16, align_bytes=DMA_ALIGN, name="raw")
-    images = node[half * IMAGES : (half + 1) * IMAGES]
-    nc.sync.dma_start(out=raw[:], in_=images.rearrange("b (p j) h w -> p b (j h w)", j=PACK))
+def load_node(nc, pool, node):
+    raw = pool.tile([P, BATCH, PACK * PIXELS], BF16, align_bytes=DMA_ALIGN, name="raw")
+    nc.sync.dma_start(out=raw[:], in_=node.rearrange("b (p j) h w -> p b (j h w)", j=PACK))
     return raw
 
 
@@ -66,7 +65,7 @@ def tile_gnn_pb_kernel(
 
     with ExitStack() as ctx:
         keep = ctx.enter_context(tc.tile_pool(name="keep", bufs=1))
-        raw_pool = ctx.enter_context(tc.tile_pool(name="raw_pool", bufs=CHUNKS))
+        raw_pool = ctx.enter_context(tc.tile_pool(name="raw_pool", bufs=NODES))
         stage = ctx.enter_context(tc.tile_pool(name="stage", bufs=4))
         part_pool = ctx.enter_context(tc.tile_pool(name="part_pool", bufs=4))
         results = ctx.enter_context(tc.tile_pool(name="results", bufs=RESULT_BUFS))
@@ -80,13 +79,12 @@ def tile_gnn_pb_kernel(
         raw_parent = {}
         raw_part = {}
         loaded_weights = set()
-        for r in range(ROUNDS):
-            part, half = divmod(r, HALVES)
+        for part in range(PARTS):
             parent = PARENT_OF_PART[part]
             weight = WEIGHT_OF_PART[part]
-            if (parent, half) not in raw_parent:
-                raw_parent[(parent, half)] = load_half_node(nc, raw_pool, h_nodes[parent], half)
-            raw_part[r] = load_half_node(nc, raw_pool, p_nodes[part], half)
+            if parent not in raw_parent:
+                raw_parent[parent] = load_node(nc, raw_pool, h_nodes[parent])
+            raw_part[part] = load_node(nc, raw_pool, p_nodes[part])
             if weight not in loaded_weights:
                 loaded_weights.add(weight)
                 for quadrant in range(QUADRANTS):
@@ -137,6 +135,7 @@ def tile_gnn_pb_kernel(
         to_quantise = {}
         parent_codes = {}
         part_codes = {}
+        part_result = {}
 
         def sort_weight(weight):
             nc.vector.tensor_copy(
@@ -156,17 +155,19 @@ def tile_gnn_pb_kernel(
                 h_codes = keep.tile([P, COLS], U32, align_bytes=64, name="h_codes_%d_%d" % (parent, half))
                 h_scales = keep.tile([P, COLS], U8, align_bytes=64, name="h_scales_%d_%d" % (parent, half))
                 parent_codes[(parent, half)] = (h_codes, h_scales)
-                jobs.append((raw_parent[(parent, half)], h_codes, h_scales))
+                jobs.append((raw_parent[parent], h_codes, h_scales))
             p_codes = part_pool.tile([P, COLS], U32, align_bytes=64, name="p_codes")
             p_scales = part_pool.tile([P, COLS], U8, align_bytes=64, name="p_scales")
             part_codes[r] = (p_codes, p_scales)
-            jobs.append((raw_part[r], p_codes, p_scales))
+            jobs.append((raw_part[part], p_codes, p_scales))
             to_quantise[r] = []
             for raw, codes, scales in jobs:
                 grouped = stage.tile([P, COLS, PACK], BF16, align_bytes=64, name="grouped")
                 nc.vector.tensor_copy(
                     out=grouped[:].rearrange("p (b c i) j -> p b c j i", b=IMAGES, i=4),
-                    in_=raw[:].rearrange("p b (j c i) -> p b c j i", j=PACK, i=4),
+                    in_=raw[:, half * IMAGES : (half + 1) * IMAGES, :].rearrange(
+                        "p b (j c i) -> p b c j i", j=PACK, i=4
+                    ),
                 )
                 to_quantise[r].append((grouped, codes, scales))
 
@@ -182,7 +183,12 @@ def tile_gnn_pb_kernel(
             part, half = divmod(r, HALVES)
             weight = WEIGHT_OF_PART[part]
             operands = (parent_codes[(PARENT_OF_PART[part], half)], part_codes[r])
-            result = results.tile([P, IMAGES, O_SETS, PIXELS], F32, align_bytes=DMA_ALIGN, name="result")
+            if half == 0:
+                part_result[part] = results.tile(
+                    [P, BATCH, O_SETS, PIXELS], F32, align_bytes=DMA_ALIGN, name="result"
+                )
+            images = slice(half * IMAGES, (half + 1) * IMAGES)
+            result = part_result[part]
             for j in range(O_SETS):
                 channels = slice(j * P, (j + 1) * P)
                 acc = sum_banks.tile([P, COLS], F32, name="acc")
@@ -198,18 +204,23 @@ def tile_gnn_pb_kernel(
                         stop=(g == K_GROUPS - 1),
                     )
                 nc.scalar.activation(
-                    out=result[:, :, j, :],
+                    out=result[:, images, j, :],
                     in_=acc[:].rearrange("m (b s) -> m b s", b=IMAGES),
                     func=RELU,
                     bias=bn_shift[:, j, weight : weight + 1],
                     scale=bn_scale[:, j, weight : weight + 1],
                 )
-            nc.scalar.dma_start(
-                out=out[part, half * IMAGES : (half + 1) * IMAGES].rearrange(
-                    "b (m j) h w -> m b (j h w)", j=O_SETS
-                ),
-                in_=result[:].rearrange("m b j s -> m b (j s)"),
-            )
+            if part == PARTS - 1:
+                stored = images
+            elif half == HALVES - 1:
+                stored = slice(0, BATCH)
+            else:
+                stored = None
+            if stored is not None:
+                nc.scalar.dma_start(
+                    out=out[part, stored].rearrange("b (m j) h w -> m b (j h w)", j=O_SETS),
+                    in_=result[:, stored].rearrange("m b j s -> m b (j s)"),
+                )
 
         with tc.manual_schedule():
             sorted_weights = set()

@@ -35,6 +35,7 @@ BN_ROWS = 4
 
 NODES = PARTS + PARENTS
 DMA_ALIGN = 256
+PARENTS_ON_SCALAR = (0, 1)
 RESULT_BUFS = 5
 
 FLOPS = 2 * PARTS * BATCH * PIXELS * CHANNELS * (K_GROUPS * CHANNELS)
@@ -139,8 +140,8 @@ def tile_gnn_pb_kernel(
 
         def sort_weight(weight):
             nc.vector.tensor_copy(
-                out=w_scales[:, weight].rearrange("p g (j m) -> p g m j", j=O_SETS),
-                in_=arrived_scales[:, weight].rearrange("p g (m j) -> p g m j", j=O_SETS),
+                out=w_scales[:, weight].rearrange("p g (j m) -> p g j m", j=O_SETS),
+                in_=arrived_scales[:, weight].rearrange("p g (m j) -> p g j m", j=O_SETS),
             )
             nc.vector.tensor_copy(
                 out=w_words[:, weight].bitcast(I32).rearrange("p g (j m) -> p g j m", j=O_SETS),
@@ -155,15 +156,16 @@ def tile_gnn_pb_kernel(
                 h_codes = keep.tile([P, COLS], U32, align_bytes=64, name="h_codes_%d_%d" % (parent, half))
                 h_scales = keep.tile([P, COLS], U8, align_bytes=64, name="h_scales_%d_%d" % (parent, half))
                 parent_codes[(parent, half)] = (h_codes, h_scales)
-                jobs.append((raw_parent[parent], h_codes, h_scales))
+                copier = nc.scalar.copy if parent in PARENTS_ON_SCALAR else nc.vector.tensor_copy
+                jobs.append((copier, raw_parent[parent], h_codes, h_scales))
             p_codes = part_pool.tile([P, COLS], U32, align_bytes=64, name="p_codes")
             p_scales = part_pool.tile([P, COLS], U8, align_bytes=64, name="p_scales")
             part_codes[r] = (p_codes, p_scales)
-            jobs.append((raw_part[part], p_codes, p_scales))
+            jobs.append((nc.vector.tensor_copy, raw_part[part], p_codes, p_scales))
             to_quantise[r] = []
-            for raw, codes, scales in jobs:
+            for copier, raw, codes, scales in jobs:
                 grouped = stage.tile([P, COLS, PACK], BF16, align_bytes=64, name="grouped")
-                nc.vector.tensor_copy(
+                copier(
                     out=grouped[:].rearrange("p (b c i) j -> p b c j i", b=IMAGES, i=4),
                     in_=raw[:, half * IMAGES : (half + 1) * IMAGES, :].rearrange(
                         "p b (j c i) -> p b c j i", j=PACK, i=4
@@ -226,11 +228,13 @@ def tile_gnn_pb_kernel(
             sorted_weights = set()
             regroup(0)
             for r in range(ROUNDS):
-                if r + 1 < ROUNDS:
+                if r + 1 < ROUNDS - 1:
                     regroup(r + 1)
                 weight = WEIGHT_OF_PART[r // HALVES]
                 if weight not in sorted_weights:
                     sorted_weights.add(weight)
                     sort_weight(weight)
                 quantise(r)
+                if r + 1 == ROUNDS - 1:
+                    regroup(r + 1)
                 multiply_and_finish(r)

@@ -219,7 +219,7 @@ def tile_gnn_pb_kernel(
             else:
                 stored = None
             if stored is not None:
-                nc.scalar.dma_start(
+                nc.sync.dma_start(
                     out=out[part, stored].rearrange("b (m j) h w -> m b (j h w)", j=O_SETS),
                     in_=result[:, stored].rearrange("m b j s -> m b (j s)"),
                 )

@@ -31,6 +31,7 @@ HALVES = BATCH // IMAGES
 ROUNDS = PARTS * HALVES
 O_SETS = CHANNELS // P
 QUADRANTS = 4
+SCALE_ROWS = 4
 BN_ROWS = 4
 
 NODES = PARTS + PARENTS
@@ -88,11 +89,11 @@ def tile_gnn_pb_kernel(
             raw_part[part] = load_node(nc, raw_pool, p_nodes[part])
             if weight not in loaded_weights:
                 loaded_weights.add(weight)
-                for quadrant in range(QUADRANTS):
-                    rows = weight_scales[weight][:, 4 * quadrant : 4 * quadrant + 4, :]
+                for i in range(SCALE_ROWS):
+                    rows = weight_scales[weight][:, i : QUADRANTS * SCALE_ROWS : SCALE_ROWS, :]
                     nc.sync.dma_start(
-                        out=arrived_scales[32 * quadrant : 32 * quadrant + 4, weight].bitcast(I32),
-                        in_=rows.rearrange("g r n -> r g n").bitcast(I32),
+                        out=arrived_scales[i : P : P // QUADRANTS, weight].bitcast(I32),
+                        in_=rows.rearrange("g q n -> q g n").bitcast(I32),
                     )
                 nc.sync.dma_start(
                     out=arrived_words[:, weight].bitcast(I32),

@@ -81,57 +81,66 @@ def tile_gnn_pb_kernel(
         raw_parent = {}
         raw_part = {}
         loaded_weights = set()
-        for part in range(PARTS):
-            parent = PARENT_OF_PART[part]
-            weight = WEIGHT_OF_PART[part]
-            if parent not in raw_parent:
-                raw_parent[parent] = load_node(nc, raw_pool, h_nodes[parent])
-            raw_part[part] = load_node(nc, raw_pool, p_nodes[part])
-            if weight not in loaded_weights:
-                loaded_weights.add(weight)
-                for i in range(SCALE_ROWS):
-                    rows = weight_scales[weight][:, i : QUADRANTS * SCALE_ROWS : SCALE_ROWS, :]
+        bn_rows = keep.tile([P, CHANNELS], BF16)
+        nc.vector.memset(bn_rows[:], 0.0)
+        with tc.manual_schedule(engines={mybir.EngineType.SP}):
+            for part in range(PARTS):
+                parent = PARENT_OF_PART[part]
+                weight = WEIGHT_OF_PART[part]
+                if parent not in raw_parent:
+                    raw_parent[parent] = load_node(nc, raw_pool, h_nodes[parent])
+                    if parent == 1:
+                        for bn in range(WEIGHTS):
+                            nc.sync.dma_start(
+                                out=bn_rows[bn * BN_ROWS : (bn + 1) * BN_ROWS, :], in_=batch_norms[bn]
+                            )
+                raw_part[part] = load_node(nc, raw_pool, p_nodes[part])
+                if weight not in loaded_weights:
+                    loaded_weights.add(weight)
+                    for i in range(SCALE_ROWS):
+                        rows = weight_scales[weight][:, i : QUADRANTS * SCALE_ROWS : SCALE_ROWS, :]
+                        nc.sync.dma_start(
+                            out=arrived_scales[i : P : P // QUADRANTS, weight].bitcast(I32),
+                            in_=rows.rearrange("g q n -> q g n").bitcast(I32),
+                        )
                     nc.sync.dma_start(
-                        out=arrived_scales[i : P : P // QUADRANTS, weight].bitcast(I32),
-                        in_=rows.rearrange("g q n -> q g n").bitcast(I32),
+                        out=arrived_words[:, weight].bitcast(I32),
+                        in_=weight_words[weight].rearrange("g p n t -> p g (n t)").bitcast(I32),
                     )
-                nc.sync.dma_start(
-                    out=arrived_words[:, weight].bitcast(I32),
-                    in_=weight_words[weight].rearrange("g p n t -> p g (n t)").bitcast(I32),
-                )
 
         identity = keep.tile([P, P], F32)
         make_identity(nc, identity[:])
-        bn_rows = keep.tile([P, CHANNELS], BF16)
-        nc.vector.memset(bn_rows[:], 0.0)
-        for weight in range(WEIGHTS):
-            nc.scalar.dma_start(
-                out=bn_rows[weight * BN_ROWS : (weight + 1) * BN_ROWS, :], in_=batch_norms[weight]
-            )
-        bn_sorted = keep.tile([P, O_SETS, P], F32)
-        nc.vector.tensor_copy(out=bn_sorted[:], in_=bn_rows[:].rearrange("p (m j) -> p j m", j=O_SETS))
         bn_cols = keep.tile([P, O_SETS, WEIGHTS, BN_ROWS], F32)
-        with tc.psum_pool(name="bn_bank", bufs=1) as bn_bank:
-            bn_turned = bn_bank.tile([P, O_SETS, P], F32)
+        bn_scale = keep.tile([P, O_SETS, WEIGHTS], F32)
+        bn_shift = keep.tile([P, O_SETS, WEIGHTS], F32)
+        gamma, beta, mean, var = (bn_cols[:, :, :, row] for row in range(BN_ROWS))
+
+        def turn_batch_norm():
+            bn_sorted = keep.tile([P, O_SETS, P], F32)
+            nc.vector.tensor_copy(out=bn_sorted[:], in_=bn_rows[:].rearrange("p (m j) -> p j m", j=O_SETS))
+            bn_turned = sum_banks.tile([P, O_SETS, P], F32, name="acc")
             for j in range(O_SETS):
                 nc.tensor.transpose(bn_turned[:, j, :], bn_sorted[:, j, :], identity[:])
+            return bn_turned
+
+        def deviation(bn_turned):
             nc.vector.tensor_copy(
                 out=bn_cols[:].rearrange("p j w r -> p j (w r)"),
                 in_=bn_turned[:, :, 0 : WEIGHTS * BN_ROWS],
             )
-        gamma, beta, mean, var = (bn_cols[:, :, :, row] for row in range(BN_ROWS))
-        var_eps = keep.tile([P, O_SETS, WEIGHTS], F32)
-        nc.vector.tensor_scalar_add(out=var_eps[:], in0=var, scalar1=EPS)
-        std = keep.tile([P, O_SETS, WEIGHTS], F32)
-        nc.scalar.sqrt(out=std[:], in_=var_eps[:])
-        inv_std = keep.tile([P, O_SETS, WEIGHTS], F32)
-        nc.vector.reciprocal(out=inv_std[:], in_=std[:])
-        bn_scale = keep.tile([P, O_SETS, WEIGHTS], F32)
-        nc.vector.tensor_mul(out=bn_scale[:], in0=gamma, in1=inv_std[:])
-        mean_scaled = keep.tile([P, O_SETS, WEIGHTS], F32)
-        nc.vector.tensor_mul(out=mean_scaled[:], in0=mean, in1=bn_scale[:])
-        bn_shift = keep.tile([P, O_SETS, WEIGHTS], F32)
-        nc.vector.tensor_sub(out=bn_shift[:], in0=beta, in1=mean_scaled[:])
+            var_eps = keep.tile([P, O_SETS, WEIGHTS], F32)
+            nc.vector.tensor_scalar_add(out=var_eps[:], in0=var, scalar1=EPS)
+            std = keep.tile([P, O_SETS, WEIGHTS], F32)
+            nc.scalar.sqrt(out=std[:], in_=var_eps[:])
+            return std
+
+        def scale_and_shift(std):
+            inv_std = keep.tile([P, O_SETS, WEIGHTS], F32)
+            nc.vector.reciprocal(out=inv_std[:], in_=std[:])
+            nc.vector.tensor_mul(out=bn_scale[:], in0=gamma, in1=inv_std[:])
+            mean_scaled = keep.tile([P, O_SETS, WEIGHTS], F32)
+            nc.vector.tensor_mul(out=mean_scaled[:], in0=mean, in1=bn_scale[:])
+            nc.vector.tensor_sub(out=bn_shift[:], in0=beta, in1=mean_scaled[:])
 
         sum_banks = ctx.enter_context(tc.psum_pool(name="sum_banks", bufs=2 * O_SETS))
         to_quantise = {}
@@ -235,7 +244,11 @@ def tile_gnn_pb_kernel(
                 if weight not in sorted_weights:
                     sorted_weights.add(weight)
                     sort_weight(weight)
+                if r == 0:
+                    bn_turned = turn_batch_norm()
                 quantise(r)
+                if r == 0:
+                    scale_and_shift(deviation(bn_turned))
                 if r + 1 == ROUNDS - 1:
                     regroup(r + 1)
                 multiply_and_finish(r)

@@ -176,9 +176,9 @@ def tile_gnn_pb_kernel(
             for copier, raw, codes, scales in jobs:
                 grouped = stage.tile([P, COLS, PACK], BF16, align_bytes=64, name="grouped")
                 copier(
-                    out=grouped[:].rearrange("p (b c i) j -> p b c j i", b=IMAGES, i=4),
+                    out=grouped[:].rearrange("p (b s) j -> p b s j", b=IMAGES),
                     in_=raw[:, half * IMAGES : (half + 1) * IMAGES, :].rearrange(
-                        "p b (j c i) -> p b c j i", j=PACK, i=4
+                        "p b (j s) -> p b s j", j=PACK
                     ),
                 )
                 to_quantise[r].append((grouped, codes, scales))

from contextlib import ExitStack

import concourse.mybir as mybir
from concourse.masks import make_identity

F32 = mybir.dt.float32
BF16 = mybir.dt.bfloat16
I32 = mybir.dt.int32
U32 = mybir.dt.uint32
U8 = mybir.dt.uint8
FP8X4 = mybir.dt.float8_e4m3fn_x4
RELU = mybir.ActivationFunctionType.Relu

P = 128
PACK = 4
PARTS = 7
PARENTS = 3
BATCH = 8
CHANNELS = 512
PIXELS = 128
EPS = 1e-5

PARENT_OF_PART = (0, 1, 1, 1, 1, 2, 2)
WEIGHT_OF_PART = (0, 1, 1, 1, 1, 1, 1)
WEIGHTS = 2
K_GROUPS = 2

IMAGES = 4
COLS = IMAGES * PIXELS
HALVES = BATCH // IMAGES
ROUNDS = PARTS * HALVES
O_SETS = CHANNELS // P
QUADRANTS = 4
SCALE_ROWS = 4
BN_ROWS = 4

NODES = PARTS + PARENTS
DMA_ALIGN = 256
PARENTS_ON_SCALAR = (0, 1)
RESULT_BUFS = 5

FLOPS = 2 * PARTS * BATCH * PIXELS * CHANNELS * (K_GROUPS * CHANNELS)


def load_node(nc, pool, node):
    raw = pool.tile([P, BATCH, PACK * PIXELS], BF16, align_bytes=DMA_ALIGN, name="raw")
    nc.sync.dma_start(out=raw[:], in_=node.rearrange("b (p j) h w -> p b (j h w)", j=PACK))
    return raw


def tile_gnn_pb_kernel(
    tc,
    p_nodes,
    h_nodes,
    W_decomp_half_words,
    W_decomp_half_scales,
    bn_decomp_half,
    W_bg_p_words,
    W_bg_p_scales,
    bn_bg_p,
    out,
):
    nc = tc.nc
    weight_words = (W_bg_p_words, W_decomp_half_words)
    weight_scales = (W_bg_p_scales, W_decomp_half_scales)
    batch_norms = (bn_bg_p, bn_decomp_half)

    with ExitStack() as ctx:
        keep = ctx.enter_context(tc.tile_pool(name="keep", bufs=1))
        raw_pool = ctx.enter_context(tc.tile_pool(name="raw_pool", bufs=NODES))
        stage = ctx.enter_context(tc.tile_pool(name="stage", bufs=4))
        part_pool = ctx.enter_context(tc.tile_pool(name="part_pool", bufs=4))
        results = ctx.enter_context(tc.tile_pool(name="results", bufs=RESULT_BUFS))

        arrived_words = keep.tile([P, WEIGHTS, K_GROUPS, CHANNELS], U32, align_bytes=DMA_ALIGN)
        arrived_scales = keep.tile([P, WEIGHTS, K_GROUPS, CHANNELS], U8, align_bytes=64)
        w_words = keep.tile([P, WEIGHTS, K_GROUPS, CHANNELS], U32, align_bytes=64)
        w_scales = keep.tile([P, WEIGHTS, K_GROUPS, CHANNELS], U8, align_bytes=64)
        nc.vector.memset(arrived_scales[:].bitcast(I32), 0)

        raw_parent = {}
        raw_part = {}
        loaded_weights = set()
        bn_rows = keep.tile([P, CHANNELS], BF16)
        nc.vector.memset(bn_rows[:], 0.0)
        with tc.manual_schedule(engines={mybir.EngineType.SP}):
            for part in range(PARTS):
                parent = PARENT_OF_PART[part]
                weight = WEIGHT_OF_PART[part]
                if parent not in raw_parent:
                    raw_parent[parent] = load_node(nc, raw_pool, h_nodes[parent])
                    if parent == 1:
                        for bn in range(WEIGHTS):
                            nc.sync.dma_start(
                                out=bn_rows[bn * BN_ROWS : (bn + 1) * BN_ROWS, :], in_=batch_norms[bn]
                            )
                raw_part[part] = load_node(nc, raw_pool, p_nodes[part])
                if weight not in loaded_weights:
                    loaded_weights.add(weight)
                    for i in range(SCALE_ROWS):
                        rows = weight_scales[weight][:, i : QUADRANTS * SCALE_ROWS : SCALE_ROWS, :]
                        nc.sync.dma_start(
                            out=arrived_scales[i : P : P // QUADRANTS, weight].bitcast(I32),
                            in_=rows.rearrange("g q n -> q g n").bitcast(I32),
                        )
                    nc.sync.dma_start(
                        out=arrived_words[:, weight].bitcast(I32),
                        in_=weight_words[weight].rearrange("g p n t -> p g (n t)").bitcast(I32),
                    )

        identity = keep.tile([P, P], F32)
        make_identity(nc, identity[:])
        bn_cols = keep.tile([P, O_SETS, WEIGHTS, BN_ROWS], F32)
        bn_scale = keep.tile([P, O_SETS, WEIGHTS], F32)
        bn_shift = keep.tile([P, O_SETS, WEIGHTS], F32)
        gamma, beta, mean, var = (bn_cols[:, :, :, row] for row in range(BN_ROWS))

        def turn_batch_norm():
            bn_sorted = keep.tile([P, O_SETS, P], F32)
            nc.vector.tensor_copy(out=bn_sorted[:], in_=bn_rows[:].rearrange("p (m j) -> p j m", j=O_SETS))
            bn_turned = sum_banks.tile([P, O_SETS, P], F32, name="acc")
            for j in range(O_SETS):
                nc.tensor.transpose(bn_turned[:, j, :], bn_sorted[:, j, :], identity[:])
            return bn_turned

        def deviation(bn_turned):
            nc.vector.tensor_copy(
                out=bn_cols[:].rearrange("p j w r -> p j (w r)"),
                in_=bn_turned[:, :, 0 : WEIGHTS * BN_ROWS],
            )
            var_eps = keep.tile([P, O_SETS, WEIGHTS], F32)
            nc.vector.tensor_scalar_add(out=var_eps[:], in0=var, scalar1=EPS)
            std = keep.tile([P, O_SETS, WEIGHTS], F32)
            nc.scalar.sqrt(out=std[:], in_=var_eps[:])
            return std

        def scale_and_shift(std):
            inv_std = keep.tile([P, O_SETS, WEIGHTS], F32)
            nc.vector.reciprocal(out=inv_std[:], in_=std[:])
            nc.vector.tensor_mul(out=bn_scale[:], in0=gamma, in1=inv_std[:])
            mean_scaled = keep.tile([P, O_SETS, WEIGHTS], F32)
            nc.vector.tensor_mul(out=mean_scaled[:], in0=mean, in1=bn_scale[:])
            nc.vector.tensor_sub(out=bn_shift[:], in0=beta, in1=mean_scaled[:])

        sum_banks = ctx.enter_context(tc.psum_pool(name="sum_banks", bufs=2 * O_SETS))
        to_quantise = {}
        parent_codes = {}
        part_codes = {}
        part_result = {}

        def sort_weight(weight):
            nc.vector.tensor_copy(
                out=w_scales[:, weight].rearrange("p g (j m) -> p g j m", j=O_SETS),
                in_=arrived_scales[:, weight].rearrange("p g (m j) -> p g j m", j=O_SETS),
            )
            nc.vector.tensor_copy(
                out=w_words[:, weight].bitcast(I32).rearrange("p g (j m) -> p g j m", j=O_SETS),
                in_=arrived_words[:, weight].bitcast(I32).rearrange("p g (m j) -> p g j m", j=O_SETS),
            )

        def regroup(r):
            part, half = divmod(r, HALVES)
            parent = PARENT_OF_PART[part]
            jobs = []
            if (parent, half) not in parent_codes:
                h_codes = keep.tile([P, COLS], U32, align_bytes=64, name="h_codes_%d_%d" % (parent, half))
                h_scales = keep.tile([P, COLS], U8, align_bytes=64, name="h_scales_%d_%d" % (parent, half))
                parent_codes[(parent, half)] = (h_codes, h_scales)
                copier = nc.scalar.copy if parent in PARENTS_ON_SCALAR else nc.vector.tensor_copy
                jobs.append((copier, raw_parent[parent], h_codes, h_scales))
            p_codes = part_pool.tile([P, COLS], U32, align_bytes=64, name="p_codes")
            p_scales = part_pool.tile([P, COLS], U8, align_bytes=64, name="p_scales")
            part_codes[r] = (p_codes, p_scales)
            jobs.append((nc.vector.tensor_copy, raw_part[part], p_codes, p_scales))
            to_quantise[r] = []
            for copier, raw, codes, scales in jobs:
                grouped = stage.tile([P, COLS, PACK], BF16, align_bytes=64, name="grouped")
                copier(
                    out=grouped[:].rearrange("p (b s) j -> p b s j", b=IMAGES),
                    in_=raw[:, half * IMAGES : (half + 1) * IMAGES, :].rearrange(
                        "p b (j s) -> p b s j", j=PACK
                    ),
                )
                to_quantise[r].append((grouped, codes, scales))

        def quantise(r):
            for grouped, codes, scales in to_quantise[r]:
                nc.vector.quantize_mx(
                    out=codes[:].bitcast(FP8X4),
                    scales=scales[:],
                    in_=grouped[:].rearrange("p w j -> p (w j)"),
                )

        def multiply_and_finish(r):
            part, half = divmod(r, HALVES)
            weight = WEIGHT_OF_PART[part]
            operands = (parent_codes[(PARENT_OF_PART[part], half)], part_codes[r])
            if half == 0:
                part_result[part] = results.tile(
                    [P, BATCH, O_SETS, PIXELS], F32, align_bytes=DMA_ALIGN, name="result"
                )
            images = slice(half * IMAGES, (half + 1) * IMAGES)
            result = part_result[part]
            for j in range(O_SETS):
                channels = slice(j * P, (j + 1) * P)
                acc = sum_banks.tile([P, COLS], F32, name="acc")
                for g in range(K_GROUPS):
                    codes, scales = operands[g]
                    nc.tensor.matmul_mx(
                        out=acc[:],
                        lhsT=w_words[:, weight, g, channels].bitcast(FP8X4),
                        lhsT_scale=w_scales[:, weight, g, channels],
                        rhs=codes[:].bitcast(FP8X4),
                        rhs_scale=scales[:],
                        start=(g == 0),
                        stop=(g == K_GROUPS - 1),
                    )
                nc.scalar.activation(
                    out=result[:, images, j, :],
                    in_=acc[:].rearrange("m (b s) -> m b s", b=IMAGES),
                    func=RELU,
                    bias=bn_shift[:, j, weight : weight + 1],
                    scale=bn_scale[:, j, weight : weight + 1],
                )
            if part == PARTS - 1:
                stored = images
            elif half == HALVES - 1:
                stored = slice(0, BATCH)
            else:
                stored = None
            if stored is not None:
                nc.sync.dma_start(
                    out=out[part, stored].rearrange("b (m j) h w -> m b (j h w)", j=O_SETS),
                    in_=result[:, stored].rearrange("m b j s -> m b (j s)"),
                )

        with tc.manual_schedule():
            sorted_weights = set()
            regroup(0)
            for r in range(ROUNDS):
                if r + 1 < ROUNDS - 1:
                    regroup(r + 1)
                weight = WEIGHT_OF_PART[r // HALVES]
                if weight not in sorted_weights:
                    sorted_weights.add(weight)
                    sort_weight(weight)
                if r == 0:
                    bn_turned = turn_batch_norm()
                quantise(r)
                if r == 0:
                    scale_and_shift(deviation(bn_turned))
                if r + 1 == ROUNDS - 1:
                    regroup(r + 1)
                multiply_and_finish(r)
